import numpy as np
import ml_dtypes


def mxq(x, axis, fmt="e4m3"):
    dtype, down = {"e4m3": (ml_dtypes.float8_e4m3fn, 7), "e5m2": (ml_dtypes.float8_e5m2, 14)}[fmt]
    v = np.moveaxis(np.asarray(x, np.float32).astype(ml_dtypes.bfloat16).astype(np.float64), axis, -1)
    blocks = v.reshape(v.shape[:-1] + (-1, 32))
    amax = np.abs(blocks).max(-1, keepdims=True)
    byte = np.maximum(np.where(amax > 0, np.frexp(amax)[1] - 1 + 127, 0) - down, 1)
    scale = np.exp2(byte - 127.0)
    codes = (blocks / scale).astype(np.float32).astype(dtype).astype(np.float64)
    return np.moveaxis((codes * scale).reshape(v.shape), -1, axis)


WIDE = False


def mx_kscale(k):
    if not WIDE:
        return np.ones(k)
    levels = np.array([20, -20, 10, -10, 0])
    a = np.random.permutation(np.resize(levels, k // 512 * 4)).reshape(k // 512, 4)
    idx = np.arange(k)
    return np.exp2(a[idx // 512, idx % 128 // 32])


BF16 = ml_dtypes.bfloat16


def bf(x):
    return np.asarray(x, np.float32).astype(BF16)


def f64(x):
    return np.asarray(x).astype(np.float64)


B, L1, L2, D1, D2, D3 = 4, 512, 512, 1024, 1024, 1024
T = B * L1


def setup_inputs():
    s = mx_kscale(T).reshape(B, L1, 1)
    x1 = np.random.standard_normal((B, L1, D1)) * s
    x2 = np.random.standard_normal((B, L2, D2)) + np.random.standard_normal((B, 1, D2))
    W1 = np.random.standard_normal((D3, D1)) * 0.03
    b1 = np.random.standard_normal(D3) * 0.3
    W2 = np.random.standard_normal((D3, D2)) * 0.03
    b2 = np.random.standard_normal(D3) * 0.3
    g = np.random.standard_normal((B, L1, D3)) * np.exp2(np.random.randint(-12, 1, (B, L1, 1))) / s
    return {"x1": bf(x1), "x2": bf(x2), "W1": bf(W1), "b1": bf(b1), "W2": bf(W2), "b2": bf(b2),
            "grad_out": bf(g)}


def reference(x1, x2, W1, b1, W2, b2, grad_out):
    g = f64(grad_out).reshape(T, D3)
    x = f64(x1).reshape(T, D1)
    return mxq(g, 0, "e5m2").T @ mxq(x, 0, "e4m3")

@@ -1,0 +1,170 @@
+from contextlib import ExitStack
+
+import concourse.mybir as mybir
+
+BF16 = mybir.dt.bfloat16
+F32 = mybir.dt.float32
+U32 = mybir.dt.uint32
+U8 = mybir.dt.uint8
+E4M3 = mybir.dt.float8_e4m3fn_x4
+E5M2 = mybir.dt.float8_e5m2_x4
+
+P = 128
+PACK = 4
+PASSES = 4
+HALF = 512
+FULL = 1024
+
+FLOPS = 2 * 2048 * 1024 * 1024
+BYTES = 2 * 2048 * 1024 * 2 + 1024 * 1024 * 4
+
+
+def tile_addpoolingfusion_kernel(tc, x1, x2, W1, b1, W2, b2, grad_out, out):
+    nc = tc.nc
+    xv = x1.rearrange("c (p j) d -> c p j d", j=PACK)
+    gv = grad_out.rearrange("c (p j) e -> c p j e", j=PACK)
+
+    with ExitStack() as ctx:
+        raw = ctx.enter_context(tc.tile_pool(name="raw", bufs=1))
+        grp = ctx.enter_context(tc.tile_pool(name="grp", bufs=1))
+        mx = ctx.enter_context(tc.tile_pool(name="mx", bufs=1))
+        res = ctx.enter_context(tc.tile_pool(name="res", bufs=1))
+        psum = ctx.enter_context(tc.psum_pool(name="psum", bufs=1))
+        ctx.enter_context(tc.manual_schedule())
+
+        chunks = {}
+
+        def make(key, width):
+            chunks[key] = (
+                raw.tile([P, PACK, width], BF16, name="raw_" + key),
+                grp.tile([P, width, PACK], BF16, name="grp_" + key, align_bytes=64),
+                mx.tile([P, width], U32, name="codes_" + key, align_bytes=64),
+                mx.tile([P, width], U8, name="scales_" + key, align_bytes=64),
+            )
+
+        for c in range(PASSES):
+            make("ga%d" % c, HALF)
+            make("gb%d" % c, HALF)
+            make("x%d" % c, FULL)
+
+        def load(key, src, w0, w1):
+            nc.sync.dma_start(out=chunks[key][0][:, :, w0:w1], in_=src)
+
+        def regroup(engine, key, w0, w1):
+            src = chunks[key][0][:, :, w0:w1].rearrange("p t (c i) -> p c t i", i=4)
+            dst = chunks[key][1][:, w0:w1, :].rearrange("p (c i) t -> p c t i", i=4)
+            if engine == "v":
+                nc.vector.tensor_copy(out=dst, in_=src)
+            else:
+                nc.scalar.copy(out=dst, in_=src)
+
+        def quantise(key, w0, w1):
+            fmt = E4M3 if key[0] == "x" else E5M2
+            nc.vector.quantize_mx(
+                out=chunks[key][2][:, w0:w1].bitcast(fmt),
+                scales=chunks[key][3][:, w0:w1],
+                in_=chunks[key][1][:, w0:w1, :].rearrange("p w j -> p (w j)"),
+            )
+
+        acc = {}
+
+        def mx_pass(rnd, e, h, c):
+            if c == 0:
+                acc[(e, h)] = psum.tile([P, HALF], F32, name="acc_%s%d%d" % (rnd, e, h), tag="bank%d%d" % (e, h))
+            g = chunks["g%s%d" % (rnd, c)]
+            x = chunks["x%d" % c]
+            nc.tensor.matmul_mx(
+                out=acc[(e, h)][:],
+                lhsT=g[2][:, e * P : (e + 1) * P].bitcast(E5M2),
+                lhsT_scale=g[3][:, e * P : (e + 1) * P],
+                rhs=x[2][:, h * HALF : (h + 1) * HALF].bitcast(E4M3),
+                rhs_scale=x[3][:, h * HALF : (h + 1) * HALF],
+                start=(c == 0),
+                stop=(c == PASSES - 1),
+            )
+
+        rows = {}
+
+        def empty(engine, rnd, e, h):
+            if (rnd, e) not in rows:
+                rows[(rnd, e)] = res.tile([P, FULL], F32, name="rows_%s%d" % (rnd, e))
+            dst = rows[(rnd, e)][:, h * HALF : (h + 1) * HALF]
+            if engine == "v":
+                nc.vector.tensor_copy(out=dst, in_=acc[(e, h)][:])
+            else:
+                nc.scalar.copy(out=dst, in_=acc[(e, h)][:])
+
+        def store(rnd, e):
+            r0 = (e + (4 if rnd == "b" else 0)) * P
+            nc.sync.dma_start(out=out[r0 : r0 + P, :], in_=rows[(rnd, e)][:])
+
+        load("ga0", gv[0][:, :, 0:HALF], 0, HALF)
+        load("x0", xv[0][:, :, 0:HALF], 0, HALF)
+        load("x0", xv[0][:, :, HALF:FULL], HALF, FULL)
+        for c in (1, 2):
+            load("ga%d" % c, gv[c][:, :, 0:HALF], 0, HALF)
+            load("x%d" % c, xv[c], 0, FULL)
+        load("ga3", gv[3][:, :, 0:HALF], 0, HALF)
+        load("x3", xv[3][:, :, 0:HALF], 0, HALF)
+        load("x3", xv[3][:, :, HALF:FULL], HALF, FULL)
+        for c in range(PASSES):
+            load("gb%d" % c, gv[c][:, :, HALF:FULL], 0, HALF)
+
+        for c in range(3):
+            regroup("v", "ga%d" % c, 0, 256)
+            regroup("s", "ga%d" % c, 256, 512)
+            if c > 0:
+                quantise("x%d" % (c - 1), HALF, FULL)
+                for e in range(4):
+                    mx_pass("a", e, 1, c - 1)
+            regroup("v", "x%d" % c, 0, HALF)
+            regroup("s", "x%d" % c, HALF, FULL)
+            quantise("ga%d" % c, 0, HALF)
+            quantise("x%d" % c, 0, HALF)
+            for e in range(4):
+                mx_pass("a", e, 0, c)
+
+        regroup("v", "ga3", 0, 256)
+        regroup("s", "ga3", 256, 512)
+        quantise("x2", HALF, FULL)
+        for e in range(4):
+            mx_pass("a", e, 1, 2)
+        quantise("ga3", 0, HALF)
+        regroup("v", "x3", 0, 352)
+        regroup("s", "x3", 352, 512)
+        quantise("x3", 0, HALF)
+        for e in range(4):
+            mx_pass("a", e, 0, 3)
+        regroup("v", "x3", 512, 864)
+        regroup("s", "x3", 864, 1024)
+        quantise("x3", HALF, FULL)
+        for e in range(4):
+            mx_pass("a", e, 1, 3)
+        regroup("v", "gb0", 0, 352)
+        regroup("s", "gb0", 352, 512)
+        quantise("gb0", 0, HALF)
+        for e in range(4):
+            empty("s", "a", e, 0)
+        empty("v", "a", 0, 1)
+        regroup("v", "gb1", 0, HALF)
+        empty("v", "a", 1, 1)
+        quantise("gb1", 0, HALF)
+        empty("s", "a", 2, 1)
+        empty("s", "a", 3, 1)
+        for e in range(4):
+            store("a", e)
+        regroup("s", "gb2", 0, HALF)
+        regroup("v", "gb3", 0, HALF)
+        quantise("gb2", 0, HALF)
+        quantise("gb3", 0, HALF)
+
+        for c in range(2):
+            for h in range(2):
+                for e in range(4):
+                    mx_pass("b", e, h, c)
+        for e in range(4):
+            for h in range(2):
+                mx_pass("b", e, h, 2)
+                mx_pass("b", e, h, 3)
+                empty("v" if h else "s", "b", e, h)
+            store("b", e)

@@ -30,7 +30,6 @@ def tile_addpoolingfusion_kernel(tc, x1, x2, W1, b1, W2, b2, grad_out, out):
         mx = ctx.enter_context(tc.tile_pool(name="mx", bufs=1))
         res = ctx.enter_context(tc.tile_pool(name="res", bufs=1))
         psum = ctx.enter_context(tc.psum_pool(name="psum", bufs=1))
-        ctx.enter_context(tc.manual_schedule())
 
         chunks = {}
 
@@ -94,9 +93,9 @@ def tile_addpoolingfusion_kernel(tc, x1, x2, W1, b1, W2, b2, grad_out, out):
             else:
                 nc.scalar.copy(out=dst, in_=acc[(e, h)][:])
 
-        def store(rnd, e):
+        def store(rnd, e, c0, c1):
             r0 = (e + (4 if rnd == "b" else 0)) * P
-            nc.sync.dma_start(out=out[r0 : r0 + P, :], in_=rows[(rnd, e)][:])
+            nc.sync.dma_start(out=out[r0 : r0 + P, c0:c1], in_=rows[(rnd, e)][:, c0:c1])
 
         load("ga0", gv[0][:, :, 0:HALF], 0, HALF)
         load("x0", xv[0][:, :, 0:HALF], 0, HALF)
@@ -152,7 +151,7 @@ def tile_addpoolingfusion_kernel(tc, x1, x2, W1, b1, W2, b2, grad_out, out):
         empty("s", "a", 2, 1)
         empty("s", "a", 3, 1)
         for e in range(4):
-            store("a", e)
+            store("a", e, 0, FULL)
         regroup("s", "gb2", 0, HALF)
         regroup("v", "gb3", 0, HALF)
         quantise("gb2", 0, HALF)
@@ -167,4 +166,7 @@ def tile_addpoolingfusion_kernel(tc, x1, x2, W1, b1, W2, b2, grad_out, out):
                 mx_pass("b", e, h, 2)
                 mx_pass("b", e, h, 3)
                 empty("v" if h else "s", "b", e, h)
-            store("b", e)
+                if e == 3:
+                    store("b", e, h * HALF, (h + 1) * HALF)
+            if e < 3:
+                store("b", e, 0, FULL)

@@ -129,18 +129,18 @@ def tile_addpoolingfusion_kernel(tc, x1, x2, W1, b1, W2, b2, grad_out, out):
         for e in range(4):
             mx_pass("a", e, 1, 2)
         quantise("ga3", 0, HALF)
-        regroup("v", "x3", 0, 352)
-        regroup("s", "x3", 352, 512)
+        regroup("v", "x3", 0, 288)
+        regroup("s", "x3", 288, 512)
         quantise("x3", 0, HALF)
         for e in range(4):
             mx_pass("a", e, 0, 3)
-        regroup("v", "x3", 512, 864)
-        regroup("s", "x3", 864, 1024)
+        regroup("v", "x3", 512, 800)
+        regroup("s", "x3", 800, 1024)
         quantise("x3", HALF, FULL)
         for e in range(4):
             mx_pass("a", e, 1, 3)
-        regroup("v", "gb0", 0, 352)
-        regroup("s", "gb0", 352, 512)
+        regroup("v", "gb0", 0, 240)
+        regroup("s", "gb0", 240, 512)
         quantise("gb0", 0, HALF)
         for e in range(4):
             empty("s", "a", e, 0)

@@ -14,6 +14,7 @@ PACK = 4
 PASSES = 4
 HALF = 512
 FULL = 1024
+PAD = 48
 
 FLOPS = 2 * 2048 * 1024 * 1024
 BYTES = 2 * 2048 * 1024 * 2 + 1024 * 1024 * 4
@@ -34,11 +35,12 @@ def tile_addpoolingfusion_kernel(tc, x1, x2, W1, b1, W2, b2, grad_out, out):
         chunks = {}
 
         def make(key, width):
+            pad = 0 if key[0] == "x" else PAD
             chunks[key] = (
                 raw.tile([P, PACK, width], BF16, name="raw_" + key),
                 grp.tile([P, width, PACK], BF16, name="grp_" + key, align_bytes=64),
-                mx.tile([P, width], U32, name="codes_" + key, align_bytes=64),
-                mx.tile([P, width], U8, name="scales_" + key, align_bytes=64),
+                mx.tile([P, pad + width], U32, name="codes_" + key, align_bytes=256)[:, pad : pad + width],
+                mx.tile([P, width], U8, name="scales_" + key, align_bytes=256),
             )
 
         for c in range(PASSES):

from contextlib import ExitStack

import concourse.mybir as mybir

BF16 = mybir.dt.bfloat16
F32 = mybir.dt.float32
U32 = mybir.dt.uint32
U8 = mybir.dt.uint8
E4M3 = mybir.dt.float8_e4m3fn_x4
E5M2 = mybir.dt.float8_e5m2_x4

P = 128
PACK = 4
PASSES = 4
HALF = 512
FULL = 1024
PAD = 48

FLOPS = 2 * 2048 * 1024 * 1024
BYTES = 2 * 2048 * 1024 * 2 + 1024 * 1024 * 4


def tile_addpoolingfusion_kernel(tc, x1, x2, W1, b1, W2, b2, grad_out, out):
    nc = tc.nc
    xv = x1.rearrange("c (p j) d -> c p j d", j=PACK)
    gv = grad_out.rearrange("c (p j) e -> c p j e", j=PACK)

    with ExitStack() as ctx:
        raw = ctx.enter_context(tc.tile_pool(name="raw", bufs=1))
        grp = ctx.enter_context(tc.tile_pool(name="grp", bufs=1))
        mx = ctx.enter_context(tc.tile_pool(name="mx", bufs=1))
        res = ctx.enter_context(tc.tile_pool(name="res", bufs=1))
        psum = ctx.enter_context(tc.psum_pool(name="psum", bufs=1))

        chunks = {}

        def make(key, width):
            pad = 0 if key[0] == "x" else PAD
            chunks[key] = (
                raw.tile([P, PACK, width], BF16, name="raw_" + key),
                grp.tile([P, width, PACK], BF16, name="grp_" + key, align_bytes=64),
                mx.tile([P, pad + width], U32, name="codes_" + key, align_bytes=256)[:, pad : pad + width],
                mx.tile([P, width], U8, name="scales_" + key, align_bytes=256),
            )

        for c in range(PASSES):
            make("ga%d" % c, HALF)
            make("gb%d" % c, HALF)
            make("x%d" % c, FULL)

        def load(key, src, w0, w1):
            nc.sync.dma_start(out=chunks[key][0][:, :, w0:w1], in_=src)

        def regroup(engine, key, w0, w1):
            src = chunks[key][0][:, :, w0:w1].rearrange("p t (c i) -> p c t i", i=4)
            dst = chunks[key][1][:, w0:w1, :].rearrange("p (c i) t -> p c t i", i=4)
            if engine == "v":
                nc.vector.tensor_copy(out=dst, in_=src)
            else:
                nc.scalar.copy(out=dst, in_=src)

        def quantise(key, w0, w1):
            fmt = E4M3 if key[0] == "x" else E5M2
            nc.vector.quantize_mx(
                out=chunks[key][2][:, w0:w1].bitcast(fmt),
                scales=chunks[key][3][:, w0:w1],
                in_=chunks[key][1][:, w0:w1, :].rearrange("p w j -> p (w j)"),
            )

        acc = {}

        def mx_pass(rnd, e, h, c):
            if c == 0:
                acc[(e, h)] = psum.tile([P, HALF], F32, name="acc_%s%d%d" % (rnd, e, h), tag="bank%d%d" % (e, h))
            g = chunks["g%s%d" % (rnd, c)]
            x = chunks["x%d" % c]
            nc.tensor.matmul_mx(
                out=acc[(e, h)][:],
                lhsT=g[2][:, e * P : (e + 1) * P].bitcast(E5M2),
                lhsT_scale=g[3][:, e * P : (e + 1) * P],
                rhs=x[2][:, h * HALF : (h + 1) * HALF].bitcast(E4M3),
                rhs_scale=x[3][:, h * HALF : (h + 1) * HALF],
                start=(c == 0),
                stop=(c == PASSES - 1),
            )

        rows = {}

        def empty(engine, rnd, e, h):
            if (rnd, e) not in rows:
                rows[(rnd, e)] = res.tile([P, FULL], F32, name="rows_%s%d" % (rnd, e))
            dst = rows[(rnd, e)][:, h * HALF : (h + 1) * HALF]
            if engine == "v":
                nc.vector.tensor_copy(out=dst, in_=acc[(e, h)][:])
            else:
                nc.scalar.copy(out=dst, in_=acc[(e, h)][:])

        def store(rnd, e, c0, c1):
            r0 = (e + (4 if rnd == "b" else 0)) * P
            nc.sync.dma_start(out=out[r0 : r0 + P, c0:c1], in_=rows[(rnd, e)][:, c0:c1])

        load("ga0", gv[0][:, :, 0:HALF], 0, HALF)
        load("x0", xv[0][:, :, 0:HALF], 0, HALF)
        load("x0", xv[0][:, :, HALF:FULL], HALF, FULL)
        for c in (1, 2):
            load("ga%d" % c, gv[c][:, :, 0:HALF], 0, HALF)
            load("x%d" % c, xv[c], 0, FULL)
        load("ga3", gv[3][:, :, 0:HALF], 0, HALF)
        load("x3", xv[3][:, :, 0:HALF], 0, HALF)
        load("x3", xv[3][:, :, HALF:FULL], HALF, FULL)
        for c in range(PASSES):
            load("gb%d" % c, gv[c][:, :, HALF:FULL], 0, HALF)

        for c in range(3):
            regroup("v", "ga%d" % c, 0, 256)
            regroup("s", "ga%d" % c, 256, 512)
            if c > 0:
                quantise("x%d" % (c - 1), HALF, FULL)
                for e in range(4):
                    mx_pass("a", e, 1, c - 1)
            regroup("v", "x%d" % c, 0, HALF)
            regroup("s", "x%d" % c, HALF, FULL)
            quantise("ga%d" % c, 0, HALF)
            quantise("x%d" % c, 0, HALF)
            for e in range(4):
                mx_pass("a", e, 0, c)

        regroup("v", "ga3", 0, 256)
        regroup("s", "ga3", 256, 512)
        quantise("x2", HALF, FULL)
        for e in range(4):
            mx_pass("a", e, 1, 2)
        quantise("ga3", 0, HALF)
        regroup("v", "x3", 0, 288)
        regroup("s", "x3", 288, 512)
        quantise("x3", 0, HALF)
        for e in range(4):
            mx_pass("a", e, 0, 3)
        regroup("v", "x3", 512, 800)
        regroup("s", "x3", 800, 1024)
        quantise("x3", HALF, FULL)
        for e in range(4):
            mx_pass("a", e, 1, 3)
        regroup("v", "gb0", 0, 240)
        regroup("s", "gb0", 240, 512)
        quantise("gb0", 0, HALF)
        for e in range(4):
            empty("s", "a", e, 0)
        empty("v", "a", 0, 1)
        regroup("v", "gb1", 0, HALF)
        empty("v", "a", 1, 1)
        quantise("gb1", 0, HALF)
        empty("s", "a", 2, 1)
        empty("s", "a", 3, 1)
        for e in range(4):
            store("a", e, 0, FULL)
        regroup("s", "gb2", 0, HALF)
        regroup("v", "gb3", 0, HALF)
        quantise("gb2", 0, HALF)
        quantise("gb3", 0, HALF)

        for c in range(2):
            for h in range(2):
                for e in range(4):
                    mx_pass("b", e, h, c)
        for e in range(4):
            for h in range(2):
                mx_pass("b", e, h, 2)
                mx_pass("b", e, h, 3)
                empty("v" if h else "s", "b", e, h)
                if e == 3:
                    store("b", e, h * HALF, (h + 1) * HALF)
            if e < 3:
                store("b", e, 0, FULL)
